import numpy as np
import ml_dtypes


def mxq(x, axis, fmt="e4m3"):
    dtype, down = {"e4m3": (ml_dtypes.float8_e4m3fn, 7), "e5m2": (ml_dtypes.float8_e5m2, 14)}[fmt]
    v = np.moveaxis(np.asarray(x, np.float32).astype(ml_dtypes.bfloat16).astype(np.float64), axis, -1)
    blocks = v.reshape(v.shape[:-1] + (-1, 32))
    amax = np.abs(blocks).max(-1, keepdims=True)
    byte = np.maximum(np.where(amax > 0, np.frexp(amax)[1] - 1 + 127, 0) - down, 1)
    scale = np.exp2(byte - 127.0)
    codes = (blocks / scale).astype(np.float32).astype(dtype).astype(np.float64)
    return np.moveaxis((codes * scale).reshape(v.shape), -1, axis)


WIDE = False


def mx_kscale(k):
    if not WIDE:
        return np.ones(k)
    levels = np.array([30, -30])
    if k % 512:
        return np.exp2(np.random.permutation(np.resize(levels, k // 32))).repeat(32)
    a = np.empty((k // 512, 16))
    for p in range(k // 512):
        a[p, :8] = np.random.permutation(np.resize(levels, 8))
        for g in range(8):
            far = levels[np.abs(levels - a[p, g]) >= 10]
            a[p, g + 8] = far[np.random.randint(len(far))]
    return np.exp2(a.ravel()).repeat(32)


BF16 = ml_dtypes.bfloat16


def bf(x):
    return np.asarray(x, np.float32).astype(BF16)


def f64(x):
    return np.asarray(x).astype(np.float64)


E2M1 = np.array([0.0, 0.5, 1.0, 1.5, 2.0, 3.0, 4.0, 6.0, -0.0, -0.5, -1.0, -1.5, -2.0, -3.0, -4.0, -6.0])


def pack_weight(w, fmt):
    k, n = w.shape
    w = f64(bf(w)).reshape(k // 32, 32, n)
    amax = np.abs(w).max(1)
    if fmt == "e4m3":
        byte = np.frexp(amax)[1] - 1 + 127 - 7
    else:
        mant, ex = np.frexp(amax / 6.0)
        byte = np.where(mant > 0.5, ex, ex - 1) + 127
    byte = np.clip(np.where(amax > 0, byte, 1), 1, 254)
    scaled = (w * np.exp2(127.0 - byte)[:, None, :]).reshape(k, n).astype(np.float32)
    by_word = np.ascontiguousarray(scaled.reshape(k // 512, 128, 4, n).transpose(0, 1, 3, 2))
    if fmt == "e4m3":
        words = by_word.astype(ml_dtypes.float8_e4m3fn).view(np.uint8)
    else:
        c = by_word.astype(ml_dtypes.float4_e2m1fn).view(np.uint8) & 0xF
        words = c[..., 0::2] | (c[..., 1::2] << 4)
    return np.ascontiguousarray(words), np.ascontiguousarray(byte.astype(np.uint8).reshape(k // 512, 16, n))


def unpack_weight(words, scales, fmt):
    g, p, n, _ = words.shape
    if fmt == "e4m3":
        vals = np.ascontiguousarray(words).view(ml_dtypes.float8_e4m3fn).astype(np.float64)
    else:
        nib = np.empty((g, p, n, 4), np.uint8)
        nib[..., 0::2] = words & 0xF
        nib[..., 1::2] = words >> 4
        vals = E2M1[nib]
    vals = vals * np.repeat(np.exp2(scales.astype(np.float64) - 127.0), 8, axis=1)[..., None]
    return vals.transpose(0, 1, 3, 2).reshape(g * 512, n)

def pack4(w):
    words, scales = pack_weight(w, "e2m1")
    return words.reshape(words.shape[0], 128, -1), scales


def unpack4(words, scales):
    return unpack_weight(words.reshape(words.shape[0], 128, -1, 2), scales, "e2m1")


BW, NW, WZ, WH, WW, C, H, HD = 4, 2, 2, 8, 8, 1536, 32, 48
N = WZ * WH * WW
F = 3 * H * HD
SCALE = HD ** -0.5


def axis_rope(x, axis):
    d = x.shape[-1]
    L = x.shape[axis]
    inv_freq = 1.0 / (10000.0 ** (np.arange(0, d, 2) / d))
    ang = np.arange(L)[:, None] * inv_freq
    cos = np.concatenate([np.cos(ang), np.cos(ang)], -1)
    sin = np.concatenate([np.sin(ang), np.sin(ang)], -1)
    bshape = [1] * x.ndim
    bshape[axis] = L
    bshape[-1] = d
    cos = cos.reshape(bshape)
    sin = sin.reshape(bshape)
    x1, x2 = np.split(x, 2, axis=-1)
    rot = np.concatenate([-x2, x1], axis=-1)
    return x * cos + rot * sin


def rope3(x):
    d = x.shape[-1] // 3
    xz, xh, xw = x[..., :d], x[..., d:2 * d], x[..., 2 * d:]
    return np.concatenate([axis_rope(xz, 1), axis_rope(xh, 2), axis_rope(xw, 3)], -1)


def setup_inputs():
    s = mx_kscale(C)
    x = bf(np.random.standard_normal((BW, N, C)) * s)
    w = np.random.standard_normal((F, C)) / np.sqrt(C) / s
    words, scales = pack4(np.ascontiguousarray(w.T))
    qkv_b = bf(np.random.standard_normal(F) * 0.3)
    return {"x": x,
            "qkv_w_words": words,
            "qkv_w_scales": scales,
            "qkv_b": qkv_b}


def reference(x, qkv_w_words, qkv_w_scales, qkv_b):
    y = (mxq(f64(x), 2, "e5m2") @ unpack4(qkv_w_words, qkv_w_scales)) + f64(qkv_b)
    qkv = y.reshape(BW, N, 3, H, HD).transpose(2, 0, 3, 1, 4)
    q, k, v = qkv[0], qkv[1], qkv[2]
    q = rope3(q.reshape(-1, WZ, WH, WW, HD)).reshape(BW, H, N, HD)
    k = rope3(k.reshape(-1, WZ, WH, WW, HD)).reshape(BW, H, N, HD)
    return q * SCALE, k, np.ascontiguousarray(v)

@@ -1,0 +1,305 @@
+from contextlib import ExitStack
+import math
+
+import concourse.mybir as mybir
+from concourse.masks import make_identity
+
+FLOPS = 2 * 512 * 1536 * 4608
+
+F32 = mybir.dt.float32
+BF16 = mybir.dt.bfloat16
+I32 = mybir.dt.int32
+U32 = mybir.dt.uint32
+U8 = mybir.dt.uint8
+E5X4 = mybir.dt.float8_e5m2_x4
+E2X4 = mybir.dt.float4_e2m1fn_x4
+ALU = mybir.AluOpType
+ACT = mybir.ActivationFunctionType
+
+P = 128
+NT = 4
+NG = 3
+HD = 48
+NH = 32
+JW = NH * HD
+HEADS = ((0, 10), (10, 21), (21, 32))
+Q_SCALE = HD ** -0.5
+
+
+def tile_windowattention_pa_kernel(tc, x, qkv_w_words, qkv_w_scales, qkv_b, out_0, out_1, out_2):
+    nc = tc.nc
+    outs = (out_0, out_1, out_2)
+
+    with ExitStack() as ctx:
+        const = ctx.enter_context(tc.tile_pool(name="const", bufs=1))
+        work = ctx.enter_context(tc.tile_pool(name="work", bufs=1))
+        psum = ctx.enter_context(tc.psum_pool(name="psum", bufs=1))
+        ctx.enter_context(tc.manual_schedule())
+
+        def bank(tag, bufs):
+            t_ps = psum.tile([P, 512], F32, name=tag, tag=tag, bufs=bufs)
+            return t_ps
+
+        x_all = const.tile([P, NT, 1536], BF16, name="x_all", align_bytes=64)
+        for b in range(4):
+            nc.sync.dma_start(out=x_all[b:P:4, :, :], in_=x[b].rearrange("(q t) c -> q t c", t=NT))
+
+        mi = const.tile([P, 1], I32, name="mi")
+        nc.gpsimd.iota(mi[:], pattern=[[0, 1]], base=0, channel_multiplier=1)
+        zero1 = const.tile([P, 1], F32, name="zero1")
+        nc.gpsimd.memset(zero1[:], 0.0)
+        warm = const.tile([P, 1], F32, name="warm")
+        nc.scalar.activation(out=warm[:], in_=zero1[:], func=ACT.Sin)
+
+        brow = const.tile([P, 512], BF16, name="brow")
+        bvr = const.tile([P, P], BF16, name="bvr")
+        nc.gpsimd.memset(brow[:], 0.0)
+        nc.gpsimd.memset(bvr[:], 0.0)
+        nc.scalar.dma_start(out=brow[0:6, :], in_=qkv_b[0 : 2 * JW].rearrange("(c n) -> c n", n=512))
+        nc.scalar.dma_start(out=bvr[0:12, :], in_=qkv_b[2 * JW : 3 * JW].rearrange("(c n) -> c n", n=P))
+
+        wq = []
+        ws = []
+        for j in range(3):
+            wq_j = []
+            for cl in range(3):
+                wq_jc = const.tile([P, NG, 1024], U8, name="wq%d%d" % (j, cl), align_bytes=64)
+                wq_j.append(wq_jc)
+            ws_j = const.tile([P, NG, JW], U8, name="ws%d" % j, align_bytes=64)
+            wq.append(wq_j)
+            ws.append(ws_j)
+
+        def load_w(j):
+            for quad in range(4):
+                nc.sync.dma_start(
+                    out=ws[j][32 * quad : 32 * quad + 4, :, :].bitcast(I32),
+                    in_=qkv_w_scales[:, 4 * quad : 4 * quad + 4, JW * j : JW * (j + 1)].rearrange("g r n -> r g n").bitcast(I32),
+                )
+            for cl in range(3):
+                c0 = 2 * JW * j + 1024 * cl
+                nc.sync.dma_start(
+                    out=wq[j][cl][:].bitcast(I32),
+                    in_=qkv_w_words[:, :, c0 : c0 + 1024].rearrange("g p n -> p g n").bitcast(I32),
+                )
+
+        nc.vector.memset(ws[0][:].rearrange("p g n -> p (g n)").bitcast(I32), 0)
+        load_w(0)
+
+        identb = const.tile([P, P], BF16, name="identb")
+        make_identity(nc, identb[:])
+        ident = const.tile([P, P], F32, name="ident")
+        make_identity(nc, ident[:])
+        nc.gpsimd.memset(ws[2][:].rearrange("p g n -> p (g n)").bitcast(F32), 0.0)
+        load_w(2)
+        nc.gpsimd.memset(ws[1][:].rearrange("p g n -> p (g n)").bitcast(F32), 0.0)
+        load_w(1)
+
+        pint = const.tile([P, 3], I32, name="pint")
+        nc.vector.tensor_scalar(out=pint[:, 0:1], in0=mi[:], scalar1=6, scalar2=None, op0=ALU.logical_shift_right)
+        nc.vector.tensor_scalar(out=pint[:, 1:2], in0=mi[:], scalar1=3, scalar2=7, op0=ALU.logical_shift_right, op1=ALU.bitwise_and)
+        nc.vector.tensor_scalar(out=pint[:, 2:3], in0=mi[:], scalar1=4, scalar2=None, op0=ALU.bitwise_and)
+        pos = const.tile([P, 6], F32, name="pos")
+        nc.vector.tensor_copy(out=pos[:, 0:3], in_=pint[:])
+        for t in range(1, NT):
+            nc.vector.tensor_scalar(out=pos[:, 2 + t : 3 + t], in0=pos[:, 2:3], scalar1=float(t), scalar2=None, op0=ALU.add)
+        arg = const.tile([P, 2, 6, 8], F32, name="arg")
+        for i in range(8):
+            nc.vector.tensor_scalar(out=arg[:, 0, :, i], in0=pos[:], scalar1=10000.0 ** (-i / 8.0), scalar2=None, op0=ALU.mult)
+        nc.vector.tensor_scalar(out=arg[:, 1], in0=arg[:, 0], scalar1=math.pi / 2.0, scalar2=None, op0=ALU.add)
+        wrap = const.tile([P, 2, 6, 8], F32, name="wrap")
+        nc.vector.tensor_scalar(out=wrap[:], in0=arg[:], scalar1=math.pi, scalar2=-2.0 * math.pi, op0=ALU.is_gt, op1=ALU.mult)
+        nc.vector.tensor_tensor(out=arg[:], in0=arg[:], in1=wrap[:], op=ALU.add)
+        trig = const.tile([P, 2, 6, 8], F32, name="trig")
+        nc.scalar.activation(out=trig[:], in_=arg[:], func=ACT.Sin)
+
+        tab = const.tile([P, 2, NT, HD], F32, name="tab")
+        for cs in range(2):
+            view = tab[:, cs].rearrange("p t (a h i) -> p t a h i", a=3, h=2)
+            src = trig[:, 1 - cs]
+            for hh in range(2):
+                f = -1.0 if (cs == 1 and hh == 1) else 1.0
+                nc.gpsimd.tensor_scalar(
+                    out=view[:, :, 0:2, hh, :],
+                    in0=src[:, 0:2, :].unsqueeze(1).to_broadcast([P, NT, 2, 8]),
+                    scalar1=f, scalar2=0.0, op0=ALU.mult, op1=ALU.add,
+                )
+                nc.gpsimd.tensor_scalar(
+                    out=view[:, :, 2, hh, :], in0=src[:, 2:6, :],
+                    scalar1=f, scalar2=0.0, op0=ALU.mult, op1=ALU.add,
+                )
+
+        bias_sb = const.tile([P, 2 * JW], F32, name="bias_sb")
+        bcol = const.tile([P, 12], F32, name="bcol")
+        head_tags = (("acc", 4), ("acc", 4), ("acc", 4), ("acc", 4), ("vacc", 2), ("vacc", 2))
+        for c in range(6):
+            pb = bank(head_tags[c][0], head_tags[c][1])
+            nc.tensor.matmul(pb[:], lhsT=identb[:, c : c + 1].to_broadcast([P, P]), rhs=brow[:], start=True, stop=True)
+            nc.scalar.activation(out=bias_sb[:, 512 * c : 512 * (c + 1)], in_=pb[:], func=ACT.Copy, scale=(Q_SCALE if c < 3 else 1.0))
+        pbc = bank("pt", 1)
+        nc.tensor.matmul(pbc[:, 0:16], lhsT=bvr[:], rhs=identb[:, 0:16], start=True, stop=True)
+        nc.scalar.copy(out=bcol[:], in_=pbc[:, 0:12])
+
+        xw = x_all[:].rearrange("p t c -> p (t c)").bitcast(F32)
+        xc = const.tile([P, NG * NT * P], U32, name="xc", align_bytes=64)
+        xs = const.tile([P, NG * NT * P], U8, name="xs", align_bytes=64)
+        grps = []
+
+        def quantise(k):
+            s0 = (k % NG) * NT + 2 * (k // NG)
+            nc.vector.quantize_mx(
+                out=xc[:, s0 * P : (s0 + 2) * P].bitcast(E5X4),
+                scales=xs[:, s0 * P : (s0 + 2) * P],
+                in_=grps[k][:],
+            )
+
+        for k in range(6):
+            tp = k // NG
+            g = k % NG
+            xt = bank("acc", 4)
+            xt4 = xt[:].rearrange("p (l u m) -> p l u m", l=2, u=2)
+            for l in range(2):
+                base = (2 * tp + l) * 768 + 256 * g
+                for u in range(2):
+                    nc.tensor.transpose(xt4[:, l, u, :], xw[:, base + u : base + 256 : 2], ident[:])
+            grp = work.tile([P, 1024], BF16, name="grp", tag="grp", bufs=3, align_bytes=64)
+            grps.append(grp)
+            grp_w = grp[:].bitcast(F32).rearrange("p (l m u) -> p l m u", l=2, u=2)
+            xt_v = xt[:].rearrange("p (l u m) -> p l m u", l=2, u=2)
+            if k % 2 == 0:
+                nc.scalar.copy(out=grp_w, in_=xt_v)
+            else:
+                nc.vector.tensor_copy(out=grp_w, in_=xt_v)
+            if k > 0:
+                quantise(k - 1)
+        quantise(5)
+
+        tab2 = tab[:].rearrange("p c t e -> p (c t e)")
+        ptmp = bank("pt", 1)
+        for k in range(3):
+            nc.tensor.transpose(ptmp[:, P * k : P * (k + 1)], tab2[:, P * k : P * (k + 1)], ident[:])
+        tabT = const.tile([P, 3 * P], F32, name="tabT")
+        nc.scalar.copy(out=tabT[:], in_=ptmp[:, 0 : 3 * P])
+        tabp = bank("tabp", 1)
+        for k in range(3):
+            nc.tensor.transpose(tabp[:, P * k : P * (k + 1)], tabT[:, P * k : P * (k + 1)], ident[:])
+        tabp_v = tabp[:, 0 : 3 * P].rearrange("p (c t e) -> p c t e", c=2, t=NT)
+
+        def qk_group(j, cl, t):
+            acc = bank("acc", 4)
+            for g in range(NG):
+                s = g * NT + t
+                nc.tensor.matmul_mx(
+                    out=acc[:],
+                    lhsT=xc[:, s * P : (s + 1) * P].bitcast(E5X4),
+                    lhsT_scale=xs[:, s * P : (s + 1) * P],
+                    rhs=wq[j][cl][:, g, :].bitcast(E2X4),
+                    rhs_scale=ws[j][:, g, 512 * cl : 512 * (cl + 1)],
+                    start=(g == 0),
+                    stop=(g == NG - 1),
+                )
+            return acc
+
+        def store(j, src, h0, nh):
+            for b in range(4):
+                nc.sync.dma_start(
+                    out=outs[j][b, h0 : h0 + nh].rearrange("h (q t) e -> q h (t e)", t=NT),
+                    in_=src[b:P:4, 0:nh].rearrange("p h t e -> p h (t e)"),
+                )
+
+        vts = {}
+        ovs = {}
+
+        def v_product(c):
+            vacc = bank("vacc", 2)
+            for g in range(NG):
+                nc.tensor.matmul_mx(
+                    out=vacc[:],
+                    lhsT=wq[2][c // 4][:, g, 256 * (c % 4) : 256 * (c % 4 + 1)].bitcast(E2X4),
+                    lhsT_scale=ws[2][:, g, P * c : P * (c + 1)],
+                    rhs=xc[:, g * 512 : (g + 1) * 512].bitcast(E5X4),
+                    rhs_scale=xs[:, g * 512 : (g + 1) * 512],
+                    start=(g == 0),
+                    stop=(g == NG - 1),
+                )
+            vt = work.tile([P, 512], F32, name="vt", tag="vt", bufs=2)
+            nc.scalar.activation(out=vt[:], in_=vacc[:], func=ACT.Identity, bias=bcol[:, c : c + 1], scale=1.0)
+            vts[c] = vt
+
+        def v_back(c):
+            pt = bank("pt", 1)
+            for t in range(NT):
+                nc.tensor.transpose(pt[:, P * t : P * (t + 1)], vts[c][:, P * t : P * (t + 1)], ident[:])
+            if c % 3 == 0:
+                o_v = work.tile([P, 8, NT, HD], F32, name="o_v", tag="o_v", bufs=2)
+                ovs[c // 3] = o_v
+            o_v = ovs[c // 3]
+            pt_v = pt[:].rearrange("p (t f) -> p t f", t=NT)
+            col = P * (c % 3)
+            end = col + P
+            while col < end:
+                h = col // HD
+                e0 = col % HD
+                a0 = col - P * (c % 3)
+                if e0 == 0 and end - col >= HD:
+                    nh = (end - col) // HD
+                    n = nh * HD
+                    nc.scalar.copy(
+                        out=o_v[:, h : h + nh].rearrange("p h t e -> p t h e"),
+                        in_=pt_v[:, :, a0 : a0 + n].rearrange("p t (h e) -> p t h e", e=HD),
+                    )
+                else:
+                    n = min(HD - e0, end - col)
+                    nc.scalar.copy(out=o_v[:, h, :, e0 : e0 + n], in_=pt_v[:, :, a0 : a0 + n])
+                col += n
+            if c % 3 == 2:
+                store(2, o_v, 8 * (c // 3), 8)
+
+        for unit in range(6):
+            j = unit // 3
+            cl = unit % 3
+            if cl == 0:
+                y_t = work.tile([P, NT, JW], F32, name="y_t", tag="y_t", bufs=1)
+            for t in range(NT):
+                acc = qk_group(j, cl, t)
+                y_out = y_t[:, t, 512 * cl : 512 * (cl + 1)]
+                b_in = bias_sb[:, JW * j + 512 * cl : JW * j + 512 * (cl + 1)]
+                if j == 0:
+                    nc.vector.scalar_tensor_tensor(out=y_out, in0=acc[:], scalar=Q_SCALE, in1=b_in, op0=ALU.mult, op1=ALU.add)
+                else:
+                    nc.vector.tensor_tensor(out=y_out, in0=acc[:], in1=b_in, op=ALU.add)
+                if t == 0:
+                    v_product(2 * unit)
+                elif t == 1:
+                    if unit > 0:
+                        v_back(2 * unit - 1)
+                elif t == 2:
+                    v_product(2 * unit + 1)
+                else:
+                    v_back(2 * unit)
+            h0, h1 = HEADS[cl]
+            nh = h1 - h0
+            y_v = y_t[:, :, HD * h0 : HD * h1].rearrange("p t (h e) -> p t h e", e=HD)
+            a_t = work.tile([P, 11, NT, HD], F32, name="a_t", tag="a_t", bufs=4)
+            b_t = work.tile([P, 11, NT, HD], F32, name="b_t", tag="b_t", bufs=3)
+            nc.vector.tensor_tensor(
+                out=a_t[:, 0:nh].rearrange("p h t e -> p t h e"), in0=y_v,
+                in1=tabp_v[:, 0].unsqueeze(2).to_broadcast([P, NT, nh, HD]), op=ALU.mult,
+            )
+            nc.vector.tensor_tensor(
+                out=b_t[:, 0:nh].rearrange("p h t e -> p t h e"), in0=y_v,
+                in1=tabp_v[:, 1].unsqueeze(2).to_broadcast([P, NT, nh, HD]), op=ALU.mult,
+            )
+            if unit < 5:
+                a_v = a_t[:, 0:nh].rearrange("p h t (a s i) -> p (h t a) s i", a=3, s=2)
+                b_v = b_t[:, 0:nh].rearrange("p h t (a s i) -> p (h t a) s i", a=3, s=2)
+                for hh in range(2):
+                    nc.gpsimd.tensor_tensor(out=a_v[:, :, hh, :], in0=a_v[:, :, hh, :], in1=b_v[:, :, 1 - hh, :], op=ALU.add)
+                store(j, a_t, h0, nh)
+            else:
+                v_back(11)
+                for (p0, p1) in ((0, 6), (6, 11)):
+                    a_v = a_t[:, p0:p1].rearrange("p h t (a s i) -> p (h t a) s i", a=3, s=2)
+                    b_v = b_t[:, p0:p1].rearrange("p h t (a s i) -> p (h t a) s i", a=3, s=2)
+                    for hh in range(2):
+                        nc.vector.tensor_tensor(out=a_v[:, :, hh, :], in0=a_v[:, :, hh, :], in1=b_v[:, :, 1 - hh, :], op=ALU.add)
+                    store(j, a_t[:, p0:p1], h0 + p0, p1 - p0)

@@ -40,23 +40,13 @@ def tile_windowattention_pa_kernel(tc, x, qkv_w_words, qkv_w_scales, qkv_b, out_
             t_ps = psum.tile([P, 512], F32, name=tag, tag=tag, bufs=bufs)
             return t_ps
 
-        x_all = const.tile([P, NT, 1536], BF16, name="x_all", align_bytes=64)
-        for b in range(4):
-            nc.sync.dma_start(out=x_all[b:P:4, :, :], in_=x[b].rearrange("(q t) c -> q t c", t=NT))
+        x_sb = []
+        for t in range(NT):
+            x_t = const.tile([P, 1536], BF16, name="x_sb%d" % t, align_bytes=64)
+            x_sb.append(x_t)
 
-        mi = const.tile([P, 1], I32, name="mi")
-        nc.gpsimd.iota(mi[:], pattern=[[0, 1]], base=0, channel_multiplier=1)
-        zero1 = const.tile([P, 1], F32, name="zero1")
-        nc.gpsimd.memset(zero1[:], 0.0)
-        warm = const.tile([P, 1], F32, name="warm")
-        nc.scalar.activation(out=warm[:], in_=zero1[:], func=ACT.Sin)
-
-        brow = const.tile([P, 512], BF16, name="brow")
-        bvr = const.tile([P, P], BF16, name="bvr")
-        nc.gpsimd.memset(brow[:], 0.0)
-        nc.gpsimd.memset(bvr[:], 0.0)
-        nc.scalar.dma_start(out=brow[0:6, :], in_=qkv_b[0 : 2 * JW].rearrange("(c n) -> c n", n=512))
-        nc.scalar.dma_start(out=bvr[0:12, :], in_=qkv_b[2 * JW : 3 * JW].rearrange("(c n) -> c n", n=P))
+        def load_x(t):
+            nc.sync.dma_start(out=x_sb[t][:], in_=x.rearrange("b (q t) c -> (b q) t c", t=NT)[:, t, :])
 
         wq = []
         ws = []
@@ -69,30 +59,49 @@ def tile_windowattention_pa_kernel(tc, x, qkv_w_words, qkv_w_scales, qkv_b, out_
             wq.append(wq_j)
             ws.append(ws_j)
 
-        def load_w(j):
+        def load_scales(j):
             for quad in range(4):
                 nc.sync.dma_start(
                     out=ws[j][32 * quad : 32 * quad + 4, :, :].bitcast(I32),
                     in_=qkv_w_scales[:, 4 * quad : 4 * quad + 4, JW * j : JW * (j + 1)].rearrange("g r n -> r g n").bitcast(I32),
                 )
-            for cl in range(3):
-                c0 = 2 * JW * j + 1024 * cl
-                nc.sync.dma_start(
-                    out=wq[j][cl][:].bitcast(I32),
-                    in_=qkv_w_words[:, :, c0 : c0 + 1024].rearrange("g p n -> p g n").bitcast(I32),
-                )
 
-        nc.vector.memset(ws[0][:].rearrange("p g n -> p (g n)").bitcast(I32), 0)
-        load_w(0)
+        def load_codes(j, cl):
+            c0 = 2 * JW * j + 1024 * cl
+            nc.sync.dma_start(
+                out=wq[j][cl][:].bitcast(I32),
+                in_=qkv_w_words[:, :, c0 : c0 + 1024].rearrange("g p n -> p g n").bitcast(I32),
+            )
 
-        identb = const.tile([P, P], BF16, name="identb")
-        make_identity(nc, identb[:])
+        def zero_plane(j):
+            nc.vector.memset(ws[j][:].rearrange("p g n -> p (g n)").bitcast(I32), 0)
+
+        mi = const.tile([P, 1], I32, name="mi")
+        zero1 = const.tile([P, 1], F32, name="zero1")
+        warm = const.tile([P, 1], F32, name="warm")
+        brow = const.tile([P, 512], BF16, name="brow")
+        bvr = const.tile([P, P], BF16, name="bvr")
         ident = const.tile([P, P], F32, name="ident")
+        identb = const.tile([P, P], BF16, name="identb")
+
+        nc.gpsimd.memset(brow[:], 0.0)
+        nc.gpsimd.memset(bvr[:], 0.0)
+        nc.scalar.dma_start(out=brow[0:6, :], in_=qkv_b[0 : 2 * JW].rearrange("(c n) -> c n", n=512))
+        nc.scalar.dma_start(out=bvr[0:12, :], in_=qkv_b[2 * JW : 3 * JW].rearrange("(c n) -> c n", n=P))
+        load_x(0)
+        load_x(1)
+        load_codes(0, 0)
+        zero_plane(0)
+        load_scales(0)
+        load_x(2)
+        load_x(3)
+        load_codes(0, 1)
+        load_codes(2, 0)
+        nc.gpsimd.iota(mi[:], pattern=[[0, 1]], base=0, channel_multiplier=1)
+        nc.gpsimd.memset(zero1[:], 0.0)
+        nc.scalar.activation(out=warm[:], in_=zero1[:], func=ACT.Sin)
         make_identity(nc, ident[:])
-        nc.gpsimd.memset(ws[2][:].rearrange("p g n -> p (g n)").bitcast(F32), 0.0)
-        load_w(2)
-        nc.gpsimd.memset(ws[1][:].rearrange("p g n -> p (g n)").bitcast(F32), 0.0)
-        load_w(1)
+        make_identity(nc, identb[:])
 
         pint = const.tile([P, 3], I32, name="pint")
         nc.vector.tensor_scalar(out=pint[:, 0:1], in0=mi[:], scalar1=6, scalar2=None, op0=ALU.logical_shift_right)
@@ -109,10 +118,17 @@ def tile_windowattention_pa_kernel(tc, x, qkv_w_words, qkv_w_scales, qkv_b, out_
         wrap = const.tile([P, 2, 6, 8], F32, name="wrap")
         nc.vector.tensor_scalar(out=wrap[:], in0=arg[:], scalar1=math.pi, scalar2=-2.0 * math.pi, op0=ALU.is_gt, op1=ALU.mult)
         nc.vector.tensor_tensor(out=arg[:], in0=arg[:], in1=wrap[:], op=ALU.add)
-        trig = const.tile([P, 2, 6, 8], F32, name="trig")
-        nc.scalar.activation(out=trig[:], in_=arg[:], func=ACT.Sin)
+        zero_plane(2)
+        load_scales(2)
+        load_codes(0, 2)
+        load_codes(2, 1)
+        load_codes(2, 2)
 
+        trig = const.tile([P, 2, 6, 8], F32, name="trig")
         tab = const.tile([P, 2, NT, HD], F32, name="tab")
+        tab2 = tab[:].rearrange("p c t e -> p (c t e)")
+        tabT = const.tile([P, 3 * P], F32, name="tabT")
+        nc.scalar.activation(out=trig[:], in_=arg[:], func=ACT.Sin)
         for cs in range(2):
             view = tab[:, cs].rearrange("p t (a h i) -> p t a h i", a=3, h=2)
             src = trig[:, 1 - cs]
@@ -128,63 +144,44 @@ def tile_windowattention_pa_kernel(tc, x, qkv_w_words, qkv_w_scales, qkv_b, out_
                     scalar1=f, scalar2=0.0, op0=ALU.mult, op1=ALU.add,
                 )
 
-        bias_sb = const.tile([P, 2 * JW], F32, name="bias_sb")
-        bcol = const.tile([P, 12], F32, name="bcol")
-        head_tags = (("acc", 4), ("acc", 4), ("acc", 4), ("acc", 4), ("vacc", 2), ("vacc", 2))
-        for c in range(6):
-            pb = bank(head_tags[c][0], head_tags[c][1])
-            nc.tensor.matmul(pb[:], lhsT=identb[:, c : c + 1].to_broadcast([P, P]), rhs=brow[:], start=True, stop=True)
-            nc.scalar.activation(out=bias_sb[:, 512 * c : 512 * (c + 1)], in_=pb[:], func=ACT.Copy, scale=(Q_SCALE if c < 3 else 1.0))
-        pbc = bank("pt", 1)
-        nc.tensor.matmul(pbc[:, 0:16], lhsT=bvr[:], rhs=identb[:, 0:16], start=True, stop=True)
-        nc.scalar.copy(out=bcol[:], in_=pbc[:, 0:12])
-
-        xw = x_all[:].rearrange("p t c -> p (t c)").bitcast(F32)
         xc = const.tile([P, NG * NT * P], U32, name="xc", align_bytes=64)
         xs = const.tile([P, NG * NT * P], U8, name="xs", align_bytes=64)
-        grps = []
+        grps = {}
 
-        def quantise(k):
-            s0 = (k % NG) * NT + 2 * (k // NG)
-            nc.vector.quantize_mx(
-                out=xc[:, s0 * P : (s0 + 2) * P].bitcast(E5X4),
-                scales=xs[:, s0 * P : (s0 + 2) * P],
-                in_=grps[k][:],
-            )
+        def transpose_x(t, tag, bufs):
+            grp = work.tile([P, NG, 512], BF16, name="grp", tag="grp", bufs=4, align_bytes=64)
+            grps[t] = grp
+            xw = x_sb[t][:].bitcast(F32)
+            for (g0, g1) in ((0, 2), (2, 3)):
+                xt = bank(tag, bufs)
+                for g in range(g0, g1):
+                    for u in range(2):
+                        o0 = ((g - g0) * 2 + u) * P
+                        nc.tensor.transpose(xt[:, o0 : o0 + P], xw[:, 256 * g + u : 256 * (g + 1) : 2], ident[:])
+                for g in range(g0, g1):
+                    nc.scalar.copy(
+                        out=grp[:, g, :].bitcast(F32).rearrange("p (q b u) -> p q b u", b=4, u=2),
+                        in_=xt[:, (g - g0) * 256 : (g - g0 + 1) * 256].rearrange("p (u b q) -> p q b u", u=2, b=4),
+                    )
 
-        for k in range(6):
-            tp = k // NG
-            g = k % NG
-            xt = bank("acc", 4)
-            xt4 = xt[:].rearrange("p (l u m) -> p l u m", l=2, u=2)
-            for l in range(2):
-                base = (2 * tp + l) * 768 + 256 * g
-                for u in range(2):
-                    nc.tensor.transpose(xt4[:, l, u, :], xw[:, base + u : base + 256 : 2], ident[:])
-            grp = work.tile([P, 1024], BF16, name="grp", tag="grp", bufs=3, align_bytes=64)
-            grps.append(grp)
-            grp_w = grp[:].bitcast(F32).rearrange("p (l m u) -> p l m u", l=2, u=2)
-            xt_v = xt[:].rearrange("p (l u m) -> p l m u", l=2, u=2)
-            if k % 2 == 0:
-                nc.scalar.copy(out=grp_w, in_=xt_v)
-            else:
-                nc.vector.tensor_copy(out=grp_w, in_=xt_v)
-            if k > 0:
-                quantise(k - 1)
-        quantise(5)
+        def quantise_x(t):
+            for g in range(NG):
+                s = g * NT + t
+                nc.vector.quantize_mx(
+                    out=xc[:, s * P : (s + 1) * P].bitcast(E5X4),
+                    scales=xs[:, s * P : (s + 1) * P],
+                    in_=grps[t][:, g, :],
+                )
 
-        tab2 = tab[:].rearrange("p c t e -> p (c t e)")
-        ptmp = bank("pt", 1)
-        for k in range(3):
-            nc.tensor.transpose(ptmp[:, P * k : P * (k + 1)], tab2[:, P * k : P * (k + 1)], ident[:])
-        tabT = const.tile([P, 3 * P], F32, name="tabT")
-        nc.scalar.copy(out=tabT[:], in_=ptmp[:, 0 : 3 * P])
-        tabp = bank("tabp", 1)
-        for k in range(3):
-            nc.tensor.transpose(tabp[:, P * k : P * (k + 1)], tabT[:, P * k : P * (k + 1)], ident[:])
-        tabp_v = tabp[:, 0 : 3 * P].rearrange("p (c t e) -> p c t e", c=2, t=NT)
+        bias_sb = const.tile([P, 2 * JW], F32, name="bias_sb")
+        bcol = const.tile([P, 12], F32, name="bcol")
 
-        def qk_group(j, cl, t):
+        def spread_bias(c):
+            pb = bank("acc", 4)
+            nc.tensor.matmul(pb[:], lhsT=identb[:, c : c + 1].to_broadcast([P, P]), rhs=brow[:], start=True, stop=True)
+            nc.scalar.activation(out=bias_sb[:, 512 * c : 512 * (c + 1)], in_=pb[:], func=ACT.Copy, scale=(Q_SCALE if c < 3 else 1.0))
+
+        def qk_group(y_t, j, cl, t):
             acc = bank("acc", 4)
             for g in range(NG):
                 s = g * NT + t
@@ -197,11 +194,16 @@ def tile_windowattention_pa_kernel(tc, x, qkv_w_words, qkv_w_scales, qkv_b, out_
                     start=(g == 0),
                     stop=(g == NG - 1),
                 )
-            return acc
+            y_out = y_t[:, t, 512 * cl : 512 * (cl + 1)]
+            b_in = bias_sb[:, JW * j + 512 * cl : JW * j + 512 * (cl + 1)]
+            if j == 0:
+                nc.vector.scalar_tensor_tensor(out=y_out, in0=acc[:], scalar=Q_SCALE, in1=b_in, op0=ALU.mult, op1=ALU.add)
+            else:
+                nc.vector.tensor_tensor(out=y_out, in0=acc[:], in1=b_in, op=ALU.add)
 
-        def store(j, src, h0, nh):
+        def store(eng, j, src, h0, nh):
             for b in range(4):
-                nc.sync.dma_start(
+                eng.dma_start(
                     out=outs[j][b, h0 : h0 + nh].rearrange("h (q t) e -> q h (t e)", t=NT),
                     in_=src[b:P:4, 0:nh].rearrange("p h t e -> p h (t e)"),
                 )
@@ -210,7 +212,7 @@ def tile_windowattention_pa_kernel(tc, x, qkv_w_words, qkv_w_scales, qkv_b, out_
         ovs = {}
 
         def v_product(c):
-            vacc = bank("vacc", 2)
+            vacc = bank("va", 1)
             for g in range(NG):
                 nc.tensor.matmul_mx(
                     out=vacc[:],
@@ -221,17 +223,20 @@ def tile_windowattention_pa_kernel(tc, x, qkv_w_words, qkv_w_scales, qkv_b, out_
                     start=(g == 0),
                     stop=(g == NG - 1),
                 )
-            vt = work.tile([P, 512], F32, name="vt", tag="vt", bufs=2)
+            vt = work.tile([P, 512], F32, name="vt", tag="vt", bufs=3)
             nc.scalar.activation(out=vt[:], in_=vacc[:], func=ACT.Identity, bias=bcol[:, c : c + 1], scale=1.0)
             vts[c] = vt
 
-        def v_back(c):
-            pt = bank("pt", 1)
+        def v_back_pe(c):
+            pt = bank("pt", 2)
             for t in range(NT):
                 nc.tensor.transpose(pt[:, P * t : P * (t + 1)], vts[c][:, P * t : P * (t + 1)], ident[:])
+            return pt
+
+        def v_back_out(c, pt):
             if c % 3 == 0:
-                o_v = work.tile([P, 8, NT, HD], F32, name="o_v", tag="o_v", bufs=2)
-                ovs[c // 3] = o_v
+                o_new = work.tile([P, 8, NT, HD], F32, name="o_v", tag="o_v", bufs=2)
+                ovs[c // 3] = o_new
             o_v = ovs[c // 3]
             pt_v = pt[:].rearrange("p (t f) -> p t f", t=NT)
             col = P * (c % 3)
@@ -252,54 +257,98 @@ def tile_windowattention_pa_kernel(tc, x, qkv_w_words, qkv_w_scales, qkv_b, out_
                     nc.scalar.copy(out=o_v[:, h, :, e0 : e0 + n], in_=pt_v[:, :, a0 : a0 + n])
                 col += n
             if c % 3 == 2:
-                store(2, o_v, 8 * (c // 3), 8)
+                store(nc.scalar, 2, o_v, 8 * (c // 3), 8)
 
-        for unit in range(6):
+        def v_back_pair(c):
+            pt0 = v_back_pe(c)
+            pt1 = v_back_pe(c + 1)
+            v_back_out(c, pt0)
+            v_back_out(c + 1, pt1)
+
+        def rotate(which, y_t, dst, h0, p0, p1, t0, t1):
+            nc.vector.tensor_tensor(
+                out=dst[:, p0:p1, t0:t1, :].rearrange("p h t e -> p t h e"),
+                in0=y_t[:, t0:t1, HD * (h0 + p0) : HD * (h0 + p1)].rearrange("p t (h e) -> p t h e", e=HD),
+                in1=tabp_v[:, which, t0:t1, :].unsqueeze(2).to_broadcast([P, t1 - t0, p1 - p0, HD]),
+                op=ALU.mult,
+            )
+
+        def combine(eng, a_t, b_t, p0, p1):
+            a_v = a_t[:, p0:p1].rearrange("p h t (a s i) -> p (h t a) s i", a=3, s=2)
+            b_v = b_t[:, p0:p1].rearrange("p h t (a s i) -> p (h t a) s i", a=3, s=2)
+            for hh in range(2):
+                eng.tensor_tensor(out=a_v[:, :, hh, :], in0=a_v[:, :, hh, :], in1=b_v[:, :, 1 - hh, :], op=ALU.add)
+
+        y_t = work.tile([P, NT, JW], F32, name="y_t", tag="y_t", bufs=1)
+        a_t = work.tile([P, 11, NT, HD], F32, name="a_t", tag="a_t", bufs=4)
+        b_t = work.tile([P, 11, NT, HD], F32, name="b_t", tag="b_t", bufs=3)
+        transpose_x(0, "pt", 2)
+        transpose_x(1, "acc", 4)
+        quantise_x(0)
+        quantise_x(1)
+        zero_plane(1)
+        load_scales(1)
+        for cl in range(3):
+            load_codes(1, cl)
+        spread_bias(0)
+        ptmp = bank("va", 1)
+        for k in range(3):
+            nc.tensor.transpose(ptmp[:, P * k : P * (k + 1)], tab2[:, P * k : P * (k + 1)], ident[:])
+        nc.scalar.copy(out=tabT[:], in_=ptmp[:, 0 : 3 * P])
+        qk_group(y_t, 0, 0, 0)
+        tabp = bank("tabp", 1)
+        for k in range(3):
+            nc.tensor.transpose(tabp[:, P * k : P * (k + 1)], tabT[:, P * k : P * (k + 1)], ident[:])
+        tabp_v = tabp[:, 0 : 3 * P].rearrange("p (c t e) -> p c t e", c=2, t=NT)
+        qk_group(y_t, 0, 0, 1)
+        rotate(0, y_t, a_t, 0, 0, 10, 0, 2)
+        transpose_x(2, "pt", 2)
+        transpose_x(3, "acc", 4)
+        quantise_x(2)
+        quantise_x(3)
+        rotate(1, y_t, b_t, 0, 0, 10, 0, 2)
+        qk_group(y_t, 0, 0, 2)
+        qk_group(y_t, 0, 0, 3)
+        rotate(0, y_t, a_t, 0, 0, 10, 2, 4)
+        rotate(1, y_t, b_t, 0, 0, 10, 2, 4)
+        combine(nc.gpsimd, a_t, b_t, 0, 10)
+        store(nc.sync, 0, a_t, 0, 10)
+        pbc = bank("va", 1)
+        nc.tensor.matmul(pbc[:, 0:16], lhsT=bvr[:], rhs=identb[:, 0:16], start=True, stop=True)
+        nc.scalar.copy(out=bcol[:], in_=pbc[:, 0:12])
+        v_product(0)
+        spread_bias(1)
+        v_product(1)
+
+        for unit in range(1, 6):
             j = unit // 3
             cl = unit % 3
-            if cl == 0:
+            if unit == 3:
                 y_t = work.tile([P, NT, JW], F32, name="y_t", tag="y_t", bufs=1)
             for t in range(NT):
-                acc = qk_group(j, cl, t)
-                y_out = y_t[:, t, 512 * cl : 512 * (cl + 1)]
-                b_in = bias_sb[:, JW * j + 512 * cl : JW * j + 512 * (cl + 1)]
-                if j == 0:
-                    nc.vector.scalar_tensor_tensor(out=y_out, in0=acc[:], scalar=Q_SCALE, in1=b_in, op0=ALU.mult, op1=ALU.add)
-                else:
-                    nc.vector.tensor_tensor(out=y_out, in0=acc[:], in1=b_in, op=ALU.add)
-                if t == 0:
-                    v_product(2 * unit)
-                elif t == 1:
-                    if unit > 0:
-                        v_back(2 * unit - 1)
-                elif t == 2:
-                    v_product(2 * unit + 1)
-                else:
-                    v_back(2 * unit)
+                qk_group(y_t, j, cl, t)
+            v_product(2 * unit)
+            v_back_pair(2 * unit - 2)
+            v_product(2 * unit + 1)
+            if unit < 5:
+                spread_bias(unit + 1)
+            else:
+                v_back_pair(10)
             h0, h1 = HEADS[cl]
             nh = h1 - h0
-            y_v = y_t[:, :, HD * h0 : HD * h1].rearrange("p t (h e) -> p t h e", e=HD)
             a_t = work.tile([P, 11, NT, HD], F32, name="a_t", tag="a_t", bufs=4)
             b_t = work.tile([P, 11, NT, HD], F32, name="b_t", tag="b_t", bufs=3)
-            nc.vector.tensor_tensor(
-                out=a_t[:, 0:nh].rearrange("p h t e -> p t h e"), in0=y_v,
-                in1=tabp_v[:, 0].unsqueeze(2).to_broadcast([P, NT, nh, HD]), op=ALU.mult,
-            )
-            nc.vector.tensor_tensor(
-                out=b_t[:, 0:nh].rearrange("p h t e -> p t h e"), in0=y_v,
-                in1=tabp_v[:, 1].unsqueeze(2).to_broadcast([P, NT, nh, HD]), op=ALU.mult,
-            )
             if unit < 5:
-                a_v = a_t[:, 0:nh].rearrange("p h t (a s i) -> p (h t a) s i", a=3, s=2)
-                b_v = b_t[:, 0:nh].rearrange("p h t (a s i) -> p (h t a) s i", a=3, s=2)
-                for hh in range(2):
-                    nc.gpsimd.tensor_tensor(out=a_v[:, :, hh, :], in0=a_v[:, :, hh, :], in1=b_v[:, :, 1 - hh, :], op=ALU.add)
-                store(j, a_t, h0, nh)
+                rotate(0, y_t, a_t, h0, 0, nh, 0, NT)
+                rotate(1, y_t, b_t, h0, 0, nh, 0, NT)
+                combine(nc.gpsimd, a_t, b_t, 0, nh)
+                store(nc.sync, j, a_t, h0, nh)
             else:
-                v_back(11)
-                for (p0, p1) in ((0, 6), (6, 11)):
-                    a_v = a_t[:, p0:p1].rearrange("p h t (a s i) -> p (h t a) s i", a=3, s=2)
-                    b_v = b_t[:, p0:p1].rearrange("p h t (a s i) -> p (h t a) s i", a=3, s=2)
-                    for hh in range(2):
-                        nc.vector.tensor_tensor(out=a_v[:, :, hh, :], in0=a_v[:, :, hh, :], in1=b_v[:, :, 1 - hh, :], op=ALU.add)
-                    store(j, a_t[:, p0:p1], h0 + p0, p1 - p0)
+                rotate(0, y_t, a_t, h0, 0, 6, 0, NT)
+                rotate(1, y_t, b_t, h0, 0, 6, 0, NT)
+                combine(nc.gpsimd, a_t, b_t, 0, 6)
+                store(nc.sync, j, a_t[:, 0:6], h0, 6)
+                rotate(0, y_t, a_t, h0, 6, 11, 0, NT)
+                rotate(1, y_t, b_t, h0, 6, 11, 0, NT)
+                combine(nc.vector, a_t, b_t, 6, 11)
+                store(nc.scalar, j, a_t[:, 6:11], h0 + 6, 5)

@@ -76,6 +76,12 @@ def tile_windowattention_pa_kernel(tc, x, qkv_w_words, qkv_w_scales, qkv_b, out_
         def zero_plane(j):
             nc.vector.memset(ws[j][:].rearrange("p g n -> p (g n)").bitcast(I32), 0)
 
+        def fill_plane(j):
+            nc.sync.dma_start(
+                out=ws[j][:].rearrange("p g n -> p (g n)").bitcast(I32),
+                in_=qkv_w_words[0, :, 0 : NG * JW].bitcast(I32),
+            )
+
         mi = const.tile([P, 1], I32, name="mi")
         zero1 = const.tile([P, 1], F32, name="zero1")
         warm = const.tile([P, 1], F32, name="warm")
@@ -84,6 +90,11 @@ def tile_windowattention_pa_kernel(tc, x, qkv_w_words, qkv_w_scales, qkv_b, out_
         ident = const.tile([P, P], F32, name="ident")
         identb = const.tile([P, P], BF16, name="identb")
 
+        zw = const.tile([P, 512], BF16, name="zw")
+        nc.vector.memset(zw[:], 0.0)
+        dm = bank("va", 1)
+        for k in range(5):
+            nc.tensor.matmul(dm[:], lhsT=zw[:, 0:P], rhs=zw[:], start=True, stop=True)
         nc.gpsimd.memset(brow[:], 0.0)
         nc.gpsimd.memset(bvr[:], 0.0)
         nc.scalar.dma_start(out=brow[0:6, :], in_=qkv_b[0 : 2 * JW].rearrange("(c n) -> c n", n=512))
@@ -96,7 +107,9 @@ def tile_windowattention_pa_kernel(tc, x, qkv_w_words, qkv_w_scales, qkv_b, out_
         load_x(2)
         load_x(3)
         load_codes(0, 1)
+        fill_plane(2)
         load_codes(2, 0)
+        load_codes(0, 2)
         nc.gpsimd.iota(mi[:], pattern=[[0, 1]], base=0, channel_multiplier=1)
         nc.gpsimd.memset(zero1[:], 0.0)
         nc.scalar.activation(out=warm[:], in_=zero1[:], func=ACT.Sin)
@@ -118,11 +131,11 @@ def tile_windowattention_pa_kernel(tc, x, qkv_w_words, qkv_w_scales, qkv_b, out_
         wrap = const.tile([P, 2, 6, 8], F32, name="wrap")
         nc.vector.tensor_scalar(out=wrap[:], in0=arg[:], scalar1=math.pi, scalar2=-2.0 * math.pi, op0=ALU.is_gt, op1=ALU.mult)
         nc.vector.tensor_tensor(out=arg[:], in0=arg[:], in1=wrap[:], op=ALU.add)
-        zero_plane(2)
         load_scales(2)
-        load_codes(0, 2)
         load_codes(2, 1)
         load_codes(2, 2)
+        fill_plane(1)
+        load_codes(1, 0)
 
         trig = const.tile([P, 2, 6, 8], F32, name="trig")
         tab = const.tile([P, 2, NT, HD], F32, name="tab")
@@ -176,10 +189,16 @@ def tile_windowattention_pa_kernel(tc, x, qkv_w_words, qkv_w_scales, qkv_b, out_
         bias_sb = const.tile([P, 2 * JW], F32, name="bias_sb")
         bcol = const.tile([P, 12], F32, name="bcol")
 
-        def spread_bias(c):
+        def spread_bias_pe(c):
             pb = bank("acc", 4)
             nc.tensor.matmul(pb[:], lhsT=identb[:, c : c + 1].to_broadcast([P, P]), rhs=brow[:], start=True, stop=True)
+            return pb
+
+        def spread_bias_out(c, pb):
             nc.scalar.activation(out=bias_sb[:, 512 * c : 512 * (c + 1)], in_=pb[:], func=ACT.Copy, scale=(Q_SCALE if c < 3 else 1.0))
+
+        def spread_bias(c):
+            spread_bias_out(c, spread_bias_pe(c))
 
         def qk_group(y_t, j, cl, t):
             acc = bank("acc", 4)
@@ -284,23 +303,22 @@ def tile_windowattention_pa_kernel(tc, x, qkv_w_words, qkv_w_scales, qkv_b, out_
         b_t = work.tile([P, 11, NT, HD], F32, name="b_t", tag="b_t", bufs=3)
         transpose_x(0, "pt", 2)
         transpose_x(1, "acc", 4)
+        spread_bias(0)
         quantise_x(0)
         quantise_x(1)
-        zero_plane(1)
         load_scales(1)
-        for cl in range(3):
+        for cl in range(1, 3):
             load_codes(1, cl)
-        spread_bias(0)
+        qk_group(y_t, 0, 0, 0)
         ptmp = bank("va", 1)
         for k in range(3):
             nc.tensor.transpose(ptmp[:, P * k : P * (k + 1)], tab2[:, P * k : P * (k + 1)], ident[:])
         nc.scalar.copy(out=tabT[:], in_=ptmp[:, 0 : 3 * P])
-        qk_group(y_t, 0, 0, 0)
+        qk_group(y_t, 0, 0, 1)
         tabp = bank("tabp", 1)
         for k in range(3):
             nc.tensor.transpose(tabp[:, P * k : P * (k + 1)], tabT[:, P * k : P * (k + 1)], ident[:])
         tabp_v = tabp[:, 0 : 3 * P].rearrange("p (c t e) -> p c t e", c=2, t=NT)
-        qk_group(y_t, 0, 0, 1)
         rotate(0, y_t, a_t, 0, 0, 10, 0, 2)
         transpose_x(2, "pt", 2)
         transpose_x(3, "acc", 4)

@@ -24,6 +24,7 @@ NH = 32
 JW = NH * HD
 HEADS = ((0, 10), (10, 21), (21, 32))
 Q_SCALE = HD ** -0.5
+POOL_HEADS = 3
 
 
 def tile_windowattention_pa_kernel(tc, x, qkv_w_words, qkv_w_scales, qkv_b, out_0, out_1, out_2):
@@ -292,6 +293,14 @@ def tile_windowattention_pa_kernel(tc, x, qkv_w_words, qkv_w_scales, qkv_b, out_
                 op=ALU.mult,
             )
 
+        def rotate_pool(y_t, dst, h0, p0, p1):
+            nc.gpsimd.tensor_tensor(
+                out=dst[:, p0:p1].rearrange("p h t e -> p t h e"),
+                in0=y_t[:, :, HD * (h0 + p0) : HD * (h0 + p1)].rearrange("p t (h e) -> p t h e", e=HD),
+                in1=tab[:, 1].unsqueeze(2).to_broadcast([P, NT, p1 - p0, HD]),
+                op=ALU.mult,
+            )
+
         def combine(eng, a_t, b_t, p0, p1):
             a_v = a_t[:, p0:p1].rearrange("p h t (a s i) -> p (h t a) s i", a=3, s=2)
             b_v = b_t[:, p0:p1].rearrange("p h t (a s i) -> p (h t a) s i", a=3, s=2)
@@ -357,8 +366,9 @@ def tile_windowattention_pa_kernel(tc, x, qkv_w_words, qkv_w_scales, qkv_b, out_
             a_t = work.tile([P, 11, NT, HD], F32, name="a_t", tag="a_t", bufs=4)
             b_t = work.tile([P, 11, NT, HD], F32, name="b_t", tag="b_t", bufs=3)
             if unit < 5:
+                rotate_pool(y_t, b_t, h0, nh - POOL_HEADS, nh)
                 rotate(0, y_t, a_t, h0, 0, nh, 0, NT)
-                rotate(1, y_t, b_t, h0, 0, nh, 0, NT)
+                rotate(1, y_t, b_t, h0, 0, nh - POOL_HEADS, 0, NT)
                 combine(nc.gpsimd, a_t, b_t, 0, nh)
                 store(nc.sync, j, a_t, h0, nh)
             else:

@@ -304,8 +304,11 @@ def tile_windowattention_pa_kernel(tc, x, qkv_w_words, qkv_w_scales, qkv_b, out_
         def combine(eng, a_t, b_t, p0, p1):
             a_v = a_t[:, p0:p1].rearrange("p h t (a s i) -> p (h t a) s i", a=3, s=2)
             b_v = b_t[:, p0:p1].rearrange("p h t (a s i) -> p (h t a) s i", a=3, s=2)
-            for hh in range(2):
-                eng.tensor_tensor(out=a_v[:, :, hh, :], in0=a_v[:, :, hh, :], in1=b_v[:, :, 1 - hh, :], op=ALU.add)
+            if eng is nc.gpsimd:
+                eng.tensor_tensor(out=a_v, in0=a_v, in1=b_v[:, :, ::-1, :], op=ALU.add)
+            else:
+                for hh in range(2):
+                    eng.tensor_tensor(out=a_v[:, :, hh, :], in0=a_v[:, :, hh, :], in1=b_v[:, :, 1 - hh, :], op=ALU.add)
 
         y_t = work.tile([P, NT, JW], F32, name="y_t", tag="y_t", bufs=1)
         a_t = work.tile([P, 11, NT, HD], F32, name="a_t", tag="a_t", bufs=4)

@@ -77,12 +77,6 @@ def tile_windowattention_pa_kernel(tc, x, qkv_w_words, qkv_w_scales, qkv_b, out_
         def zero_plane(j):
             nc.vector.memset(ws[j][:].rearrange("p g n -> p (g n)").bitcast(I32), 0)
 
-        def fill_plane(j):
-            nc.sync.dma_start(
-                out=ws[j][:].rearrange("p g n -> p (g n)").bitcast(I32),
-                in_=qkv_w_words[0, :, 0 : NG * JW].bitcast(I32),
-            )
-
         mi = const.tile([P, 1], I32, name="mi")
         zero1 = const.tile([P, 1], F32, name="zero1")
         warm = const.tile([P, 1], F32, name="warm")
@@ -102,15 +96,13 @@ def tile_windowattention_pa_kernel(tc, x, qkv_w_words, qkv_w_scales, qkv_b, out_
         nc.scalar.dma_start(out=bvr[0:12, :], in_=qkv_b[2 * JW : 3 * JW].rearrange("(c n) -> c n", n=P))
         load_x(0)
         load_x(1)
-        load_codes(0, 0)
         zero_plane(0)
         load_scales(0)
+        load_codes(0, 0)
         load_x(2)
         load_x(3)
         load_codes(0, 1)
-        fill_plane(2)
         load_codes(2, 0)
-        load_codes(0, 2)
         nc.gpsimd.iota(mi[:], pattern=[[0, 1]], base=0, channel_multiplier=1)
         nc.gpsimd.memset(zero1[:], 0.0)
         nc.scalar.activation(out=warm[:], in_=zero1[:], func=ACT.Sin)
@@ -132,11 +124,14 @@ def tile_windowattention_pa_kernel(tc, x, qkv_w_words, qkv_w_scales, qkv_b, out_
         wrap = const.tile([P, 2, 6, 8], F32, name="wrap")
         nc.vector.tensor_scalar(out=wrap[:], in0=arg[:], scalar1=math.pi, scalar2=-2.0 * math.pi, op0=ALU.is_gt, op1=ALU.mult)
         nc.vector.tensor_tensor(out=arg[:], in0=arg[:], in1=wrap[:], op=ALU.add)
+        zero_plane(2)
         load_scales(2)
+        load_codes(0, 2)
         load_codes(2, 1)
-        load_codes(2, 2)
-        fill_plane(1)
         load_codes(1, 0)
+        load_codes(1, 1)
+        load_codes(2, 2)
+        load_codes(1, 2)
 
         trig = const.tile([P, 2, 6, 8], F32, name="trig")
         tab = const.tile([P, 2, NT, HD], F32, name="tab")
@@ -318,9 +313,6 @@ def tile_windowattention_pa_kernel(tc, x, qkv_w_words, qkv_w_scales, qkv_b, out_
         spread_bias(0)
         quantise_x(0)
         quantise_x(1)
-        load_scales(1)
-        for cl in range(1, 3):
-            load_codes(1, cl)
         qk_group(y_t, 0, 0, 0)
         ptmp = bank("va", 1)
         for k in range(3):
@@ -336,6 +328,8 @@ def tile_windowattention_pa_kernel(tc, x, qkv_w_words, qkv_w_scales, qkv_b, out_
         transpose_x(3, "acc", 4)
         quantise_x(2)
         quantise_x(3)
+        zero_plane(1)
+        load_scales(1)
         rotate(1, y_t, b_t, 0, 0, 10, 0, 2)
         qk_group(y_t, 0, 0, 2)
         qk_group(y_t, 0, 0, 3)

@@ -92,7 +92,7 @@ def tile_windowattention_pa_kernel(tc, x, qkv_w_words, qkv_w_scales, qkv_b, out_
             nc.tensor.matmul(dm[:], lhsT=zw[:, 0:P], rhs=zw[:], start=True, stop=True)
         nc.gpsimd.memset(brow[:], 0.0)
         nc.gpsimd.memset(bvr[:], 0.0)
-        nc.scalar.dma_start(out=brow[0:6, :], in_=qkv_b[0 : 2 * JW].rearrange("(c n) -> c n", n=512))
+        nc.scalar.dma_start(out=brow[0:9, :], in_=qkv_b[0 : 3 * JW].rearrange("(c n) -> c n", n=512))
         nc.scalar.dma_start(out=bvr[0:12, :], in_=qkv_b[2 * JW : 3 * JW].rearrange("(c n) -> c n", n=P))
         load_x(0)
         load_x(1)
@@ -102,7 +102,7 @@ def tile_windowattention_pa_kernel(tc, x, qkv_w_words, qkv_w_scales, qkv_b, out_
         load_x(2)
         load_x(3)
         load_codes(0, 1)
-        load_codes(2, 0)
+        load_codes(2, 2)
         nc.gpsimd.iota(mi[:], pattern=[[0, 1]], base=0, channel_multiplier=1)
         nc.gpsimd.memset(zero1[:], 0.0)
         nc.scalar.activation(out=warm[:], in_=zero1[:], func=ACT.Sin)
@@ -127,10 +127,10 @@ def tile_windowattention_pa_kernel(tc, x, qkv_w_words, qkv_w_scales, qkv_b, out_
         zero_plane(2)
         load_scales(2)
         load_codes(0, 2)
-        load_codes(2, 1)
+        load_codes(2, 0)
         load_codes(1, 0)
+        load_codes(2, 1)
         load_codes(1, 1)
-        load_codes(2, 2)
         load_codes(1, 2)
 
         trig = const.tile([P, 2, 6, 8], F32, name="trig")
@@ -224,7 +224,40 @@ def tile_windowattention_pa_kernel(tc, x, qkv_w_words, qkv_w_scales, qkv_b, out_
                 )
 
         vts = {}
-        ovs = {}
+        o_vl = const.tile([P, 16, NT, HD], F32, name="o_vl")
+        ovs = {2: o_vl}
+        bias_vx = const.tile([P, 512], F32, name="bias_vx")
+
+        def vx_group(t, tag, bufs):
+            vacc = bank(tag, bufs)
+            for g in range(NG):
+                s = g * NT + t
+                nc.tensor.matmul_mx(
+                    out=vacc[:],
+                    lhsT=xc[:, s * P : (s + 1) * P].bitcast(E5X4),
+                    lhsT_scale=xs[:, s * P : (s + 1) * P],
+                    rhs=wq[2][2][:, g, :].bitcast(E2X4),
+                    rhs_scale=ws[2][:, g, 1024:1536],
+                    start=(g == 0),
+                    stop=(g == NG - 1),
+                )
+            nc.scalar.copy(out=o_vl[:, 5, t, 16:HD], in_=vacc[:, 0:32])
+            nc.scalar.copy(out=o_vl[:, 6:16, t, :], in_=vacc[:, 32:512].rearrange("p (h e) -> p h e", e=HD))
+
+        def vx_bias():
+            nc.gpsimd.tensor_tensor(
+                out=o_vl[:, 6:16],
+                in0=o_vl[:, 6:16],
+                in1=bias_vx[:, 32:512].rearrange("p (h e) -> p h e", e=HD).unsqueeze(2).to_broadcast([P, 10, NT, HD]),
+                op=ALU.add,
+            )
+            nc.gpsimd.tensor_tensor(
+                out=o_vl[:, 5, :, 16:HD],
+                in0=o_vl[:, 5, :, 16:HD],
+                in1=bias_vx[:, 0:32].unsqueeze(1).to_broadcast([P, NT, 32]),
+                op=ALU.add,
+            )
+            store(nc.sync, 2, o_vl[:, 6:16], 22, 10)
 
         def v_product(c):
             vacc = bank("va", 1)
@@ -249,7 +282,7 @@ def tile_windowattention_pa_kernel(tc, x, qkv_w_words, qkv_w_scales, qkv_b, out_
             return pt
 
         def v_back_out(c, pt):
-            if c % 3 == 0:
+            if c % 3 == 0 and c < 6:
                 o_new = work.tile([P, 8, NT, HD], F32, name="o_v", tag="o_v", bufs=2)
                 ovs[c // 3] = o_new
             o_v = ovs[c // 3]
@@ -273,6 +306,8 @@ def tile_windowattention_pa_kernel(tc, x, qkv_w_words, qkv_w_scales, qkv_b, out_
                 col += n
             if c % 3 == 2:
                 store(nc.scalar, 2, o_v, 8 * (c // 3), 8)
+            if c == 7:
+                store(nc.scalar, 2, o_v, 16, 6)
 
         def v_back_pair(c):
             pt0 = v_back_pe(c)
@@ -337,12 +372,11 @@ def tile_windowattention_pa_kernel(tc, x, qkv_w_words, qkv_w_scales, qkv_b, out_
         rotate(1, y_t, b_t, 0, 0, 10, 2, 4)
         combine(nc.gpsimd, a_t, b_t, 0, 10)
         store(nc.sync, 0, a_t, 0, 10)
-        pbc = bank("va", 1)
-        nc.tensor.matmul(pbc[:, 0:16], lhsT=bvr[:], rhs=identb[:, 0:16], start=True, stop=True)
-        nc.scalar.copy(out=bcol[:], in_=pbc[:, 0:12])
-        v_product(0)
+        pbv = spread_bias_pe(8)
+        nc.scalar.copy(out=bias_vx[:], in_=pbv[:])
+        vx_group(0, "va", 1)
         spread_bias(1)
-        v_product(1)
+        vx_group(1, "pt", 2)
 
         for unit in range(1, 6):
             j = unit // 3
@@ -351,19 +385,33 @@ def tile_windowattention_pa_kernel(tc, x, qkv_w_words, qkv_w_scales, qkv_b, out_
                 y_t = work.tile([P, NT, JW], F32, name="y_t", tag="y_t", bufs=1)
             for t in range(NT):
                 qk_group(y_t, j, cl, t)
-            v_product(2 * unit)
-            v_back_pair(2 * unit - 2)
-            v_product(2 * unit + 1)
-            if unit < 5:
-                spread_bias(unit + 1)
+            if unit == 1:
+                vx_group(2, "pt", 2)
+                vx_group(3, "va", 1)
+                spread_bias(2)
+            elif unit == 2:
+                pbc = bank("pt", 2)
+                nc.tensor.matmul(pbc[:, 0:16], lhsT=bvr[:], rhs=identb[:, 0:16], start=True, stop=True)
+                nc.scalar.copy(out=bcol[:], in_=pbc[:, 0:12])
+                v_product(0)
+                spread_bias(3)
+                v_product(1)
             else:
-                v_back_pair(10)
+                v_product(2 * unit - 4)
+                v_back_pair(2 * unit - 6)
+                v_product(2 * unit - 3)
+                if unit < 5:
+                    spread_bias(unit + 1)
+                else:
+                    v_back_pair(6)
             h0, h1 = HEADS[cl]
             nh = h1 - h0
             a_t = work.tile([P, 11, NT, HD], F32, name="a_t", tag="a_t", bufs=4)
             b_t = work.tile([P, 11, NT, HD], F32, name="b_t", tag="b_t", bufs=3)
             if unit < 5:
                 rotate_pool(y_t, b_t, h0, nh - POOL_HEADS, nh)
+                if unit == 2:
+                    vx_bias()
                 rotate(0, y_t, a_t, h0, 0, nh, 0, NT)
                 rotate(1, y_t, b_t, h0, 0, nh - POOL_HEADS, 0, NT)
                 combine(nc.gpsimd, a_t, b_t, 0, nh)

@@ -409,11 +409,13 @@ def tile_windowattention_pa_kernel(tc, x, qkv_w_words, qkv_w_scales, qkv_b, out_
             a_t = work.tile([P, 11, NT, HD], F32, name="a_t", tag="a_t", bufs=4)
             b_t = work.tile([P, 11, NT, HD], F32, name="b_t", tag="b_t", bufs=3)
             if unit < 5:
-                rotate_pool(y_t, b_t, h0, nh - POOL_HEADS, nh)
+                pool_heads = POOL_HEADS if unit < 3 else 0
+                if pool_heads:
+                    rotate_pool(y_t, b_t, h0, nh - pool_heads, nh)
                 if unit == 2:
                     vx_bias()
                 rotate(0, y_t, a_t, h0, 0, nh, 0, NT)
-                rotate(1, y_t, b_t, h0, 0, nh - POOL_HEADS, 0, NT)
+                rotate(1, y_t, b_t, h0, 0, nh - pool_heads, 0, NT)
                 combine(nc.gpsimd, a_t, b_t, 0, nh)
                 store(nc.sync, j, a_t, h0, nh)
             else:

from contextlib import ExitStack
import math

import concourse.mybir as mybir
from concourse.masks import make_identity

FLOPS = 2 * 512 * 1536 * 4608

F32 = mybir.dt.float32
BF16 = mybir.dt.bfloat16
I32 = mybir.dt.int32
U32 = mybir.dt.uint32
U8 = mybir.dt.uint8
E5X4 = mybir.dt.float8_e5m2_x4
E2X4 = mybir.dt.float4_e2m1fn_x4
ALU = mybir.AluOpType
ACT = mybir.ActivationFunctionType

P = 128
NT = 4
NG = 3
HD = 48
NH = 32
JW = NH * HD
HEADS = ((0, 10), (10, 21), (21, 32))
Q_SCALE = HD ** -0.5
POOL_HEADS = 3


def tile_windowattention_pa_kernel(tc, x, qkv_w_words, qkv_w_scales, qkv_b, out_0, out_1, out_2):
    nc = tc.nc
    outs = (out_0, out_1, out_2)

    with ExitStack() as ctx:
        const = ctx.enter_context(tc.tile_pool(name="const", bufs=1))
        work = ctx.enter_context(tc.tile_pool(name="work", bufs=1))
        psum = ctx.enter_context(tc.psum_pool(name="psum", bufs=1))
        ctx.enter_context(tc.manual_schedule())

        def bank(tag, bufs):
            t_ps = psum.tile([P, 512], F32, name=tag, tag=tag, bufs=bufs)
            return t_ps

        x_sb = []
        for t in range(NT):
            x_t = const.tile([P, 1536], BF16, name="x_sb%d" % t, align_bytes=64)
            x_sb.append(x_t)

        def load_x(t):
            nc.sync.dma_start(out=x_sb[t][:], in_=x.rearrange("b (q t) c -> (b q) t c", t=NT)[:, t, :])

        wq = []
        ws = []
        for j in range(3):
            wq_j = []
            for cl in range(3):
                wq_jc = const.tile([P, NG, 1024], U8, name="wq%d%d" % (j, cl), align_bytes=64)
                wq_j.append(wq_jc)
            ws_j = const.tile([P, NG, JW], U8, name="ws%d" % j, align_bytes=64)
            wq.append(wq_j)
            ws.append(ws_j)

        def load_scales(j):
            for quad in range(4):
                nc.sync.dma_start(
                    out=ws[j][32 * quad : 32 * quad + 4, :, :].bitcast(I32),
                    in_=qkv_w_scales[:, 4 * quad : 4 * quad + 4, JW * j : JW * (j + 1)].rearrange("g r n -> r g n").bitcast(I32),
                )

        def load_codes(j, cl):
            c0 = 2 * JW * j + 1024 * cl
            nc.sync.dma_start(
                out=wq[j][cl][:].bitcast(I32),
                in_=qkv_w_words[:, :, c0 : c0 + 1024].rearrange("g p n -> p g n").bitcast(I32),
            )

        def zero_plane(j):
            nc.vector.memset(ws[j][:].rearrange("p g n -> p (g n)").bitcast(I32), 0)

        mi = const.tile([P, 1], I32, name="mi")
        zero1 = const.tile([P, 1], F32, name="zero1")
        warm = const.tile([P, 1], F32, name="warm")
        brow = const.tile([P, 512], BF16, name="brow")
        bvr = const.tile([P, P], BF16, name="bvr")
        ident = const.tile([P, P], F32, name="ident")
        identb = const.tile([P, P], BF16, name="identb")

        zw = const.tile([P, 512], BF16, name="zw")
        nc.vector.memset(zw[:], 0.0)
        dm = bank("va", 1)
        for k in range(5):
            nc.tensor.matmul(dm[:], lhsT=zw[:, 0:P], rhs=zw[:], start=True, stop=True)
        nc.gpsimd.memset(brow[:], 0.0)
        nc.gpsimd.memset(bvr[:], 0.0)
        nc.scalar.dma_start(out=brow[0:9, :], in_=qkv_b[0 : 3 * JW].rearrange("(c n) -> c n", n=512))
        nc.scalar.dma_start(out=bvr[0:12, :], in_=qkv_b[2 * JW : 3 * JW].rearrange("(c n) -> c n", n=P))
        load_x(0)
        load_x(1)
        zero_plane(0)
        load_scales(0)
        load_codes(0, 0)
        load_x(2)
        load_x(3)
        load_codes(0, 1)
        load_codes(2, 2)
        nc.gpsimd.iota(mi[:], pattern=[[0, 1]], base=0, channel_multiplier=1)
        nc.gpsimd.memset(zero1[:], 0.0)
        nc.scalar.activation(out=warm[:], in_=zero1[:], func=ACT.Sin)
        make_identity(nc, ident[:])
        make_identity(nc, identb[:])

        pint = const.tile([P, 3], I32, name="pint")
        nc.vector.tensor_scalar(out=pint[:, 0:1], in0=mi[:], scalar1=6, scalar2=None, op0=ALU.logical_shift_right)
        nc.vector.tensor_scalar(out=pint[:, 1:2], in0=mi[:], scalar1=3, scalar2=7, op0=ALU.logical_shift_right, op1=ALU.bitwise_and)
        nc.vector.tensor_scalar(out=pint[:, 2:3], in0=mi[:], scalar1=4, scalar2=None, op0=ALU.bitwise_and)
        pos = const.tile([P, 6], F32, name="pos")
        nc.vector.tensor_copy(out=pos[:, 0:3], in_=pint[:])
        for t in range(1, NT):
            nc.vector.tensor_scalar(out=pos[:, 2 + t : 3 + t], in0=pos[:, 2:3], scalar1=float(t), scalar2=None, op0=ALU.add)
        arg = const.tile([P, 2, 6, 8], F32, name="arg")
        for i in range(8):
            nc.vector.tensor_scalar(out=arg[:, 0, :, i], in0=pos[:], scalar1=10000.0 ** (-i / 8.0), scalar2=None, op0=ALU.mult)
        nc.vector.tensor_scalar(out=arg[:, 1], in0=arg[:, 0], scalar1=math.pi / 2.0, scalar2=None, op0=ALU.add)
        wrap = const.tile([P, 2, 6, 8], F32, name="wrap")
        nc.vector.tensor_scalar(out=wrap[:], in0=arg[:], scalar1=math.pi, scalar2=-2.0 * math.pi, op0=ALU.is_gt, op1=ALU.mult)
        nc.vector.tensor_tensor(out=arg[:], in0=arg[:], in1=wrap[:], op=ALU.add)
        zero_plane(2)
        load_scales(2)
        load_codes(0, 2)
        load_codes(2, 0)
        load_codes(1, 0)
        load_codes(2, 1)
        load_codes(1, 1)
        load_codes(1, 2)

        trig = const.tile([P, 2, 6, 8], F32, name="trig")
        tab = const.tile([P, 2, NT, HD], F32, name="tab")
        tab2 = tab[:].rearrange("p c t e -> p (c t e)")
        tabT = const.tile([P, 3 * P], F32, name="tabT")
        nc.scalar.activation(out=trig[:], in_=arg[:], func=ACT.Sin)
        for cs in range(2):
            view = tab[:, cs].rearrange("p t (a h i) -> p t a h i", a=3, h=2)
            src = trig[:, 1 - cs]
            for hh in range(2):
                f = -1.0 if (cs == 1 and hh == 1) else 1.0
                nc.gpsimd.tensor_scalar(
                    out=view[:, :, 0:2, hh, :],
                    in0=src[:, 0:2, :].unsqueeze(1).to_broadcast([P, NT, 2, 8]),
                    scalar1=f, scalar2=0.0, op0=ALU.mult, op1=ALU.add,
                )
                nc.gpsimd.tensor_scalar(
                    out=view[:, :, 2, hh, :], in0=src[:, 2:6, :],
                    scalar1=f, scalar2=0.0, op0=ALU.mult, op1=ALU.add,
                )

        xc = const.tile([P, NG * NT * P], U32, name="xc", align_bytes=64)
        xs = const.tile([P, NG * NT * P], U8, name="xs", align_bytes=64)
        grps = {}

        def transpose_x(t, tag, bufs):
            grp = work.tile([P, NG, 512], BF16, name="grp", tag="grp", bufs=4, align_bytes=64)
            grps[t] = grp
            xw = x_sb[t][:].bitcast(F32)
            for (g0, g1) in ((0, 2), (2, 3)):
                xt = bank(tag, bufs)
                for g in range(g0, g1):
                    for u in range(2):
                        o0 = ((g - g0) * 2 + u) * P
                        nc.tensor.transpose(xt[:, o0 : o0 + P], xw[:, 256 * g + u : 256 * (g + 1) : 2], ident[:])
                for g in range(g0, g1):
                    nc.scalar.copy(
                        out=grp[:, g, :].bitcast(F32).rearrange("p (q b u) -> p q b u", b=4, u=2),
                        in_=xt[:, (g - g0) * 256 : (g - g0 + 1) * 256].rearrange("p (u b q) -> p q b u", u=2, b=4),
                    )

        def quantise_x(t):
            for g in range(NG):
                s = g * NT + t
                nc.vector.quantize_mx(
                    out=xc[:, s * P : (s + 1) * P].bitcast(E5X4),
                    scales=xs[:, s * P : (s + 1) * P],
                    in_=grps[t][:, g, :],
                )

        bias_sb = const.tile([P, 2 * JW], F32, name="bias_sb")
        bcol = const.tile([P, 12], F32, name="bcol")

        def spread_bias_pe(c):
            pb = bank("acc", 4)
            nc.tensor.matmul(pb[:], lhsT=identb[:, c : c + 1].to_broadcast([P, P]), rhs=brow[:], start=True, stop=True)
            return pb

        def spread_bias_out(c, pb):
            nc.scalar.activation(out=bias_sb[:, 512 * c : 512 * (c + 1)], in_=pb[:], func=ACT.Copy, scale=(Q_SCALE if c < 3 else 1.0))

        def spread_bias(c):
            spread_bias_out(c, spread_bias_pe(c))

        def qk_group(y_t, j, cl, t):
            acc = bank("acc", 4)
            for g in range(NG):
                s = g * NT + t
                nc.tensor.matmul_mx(
                    out=acc[:],
                    lhsT=xc[:, s * P : (s + 1) * P].bitcast(E5X4),
                    lhsT_scale=xs[:, s * P : (s + 1) * P],
                    rhs=wq[j][cl][:, g, :].bitcast(E2X4),
                    rhs_scale=ws[j][:, g, 512 * cl : 512 * (cl + 1)],
                    start=(g == 0),
                    stop=(g == NG - 1),
                )
            y_out = y_t[:, t, 512 * cl : 512 * (cl + 1)]
            b_in = bias_sb[:, JW * j + 512 * cl : JW * j + 512 * (cl + 1)]
            if j == 0:
                nc.vector.scalar_tensor_tensor(out=y_out, in0=acc[:], scalar=Q_SCALE, in1=b_in, op0=ALU.mult, op1=ALU.add)
            else:
                nc.vector.tensor_tensor(out=y_out, in0=acc[:], in1=b_in, op=ALU.add)

        def store(eng, j, src, h0, nh):
            for b in range(4):
                eng.dma_start(
                    out=outs[j][b, h0 : h0 + nh].rearrange("h (q t) e -> q h (t e)", t=NT),
                    in_=src[b:P:4, 0:nh].rearrange("p h t e -> p h (t e)"),
                )

        vts = {}
        o_vl = const.tile([P, 16, NT, HD], F32, name="o_vl")
        ovs = {2: o_vl}
        bias_vx = const.tile([P, 512], F32, name="bias_vx")

        def vx_group(t, tag, bufs):
            vacc = bank(tag, bufs)
            for g in range(NG):
                s = g * NT + t
                nc.tensor.matmul_mx(
                    out=vacc[:],
                    lhsT=xc[:, s * P : (s + 1) * P].bitcast(E5X4),
                    lhsT_scale=xs[:, s * P : (s + 1) * P],
                    rhs=wq[2][2][:, g, :].bitcast(E2X4),
                    rhs_scale=ws[2][:, g, 1024:1536],
                    start=(g == 0),
                    stop=(g == NG - 1),
                )
            nc.scalar.copy(out=o_vl[:, 5, t, 16:HD], in_=vacc[:, 0:32])
            nc.scalar.copy(out=o_vl[:, 6:16, t, :], in_=vacc[:, 32:512].rearrange("p (h e) -> p h e", e=HD))

        def vx_bias():
            nc.gpsimd.tensor_tensor(
                out=o_vl[:, 6:16],
                in0=o_vl[:, 6:16],
                in1=bias_vx[:, 32:512].rearrange("p (h e) -> p h e", e=HD).unsqueeze(2).to_broadcast([P, 10, NT, HD]),
                op=ALU.add,
            )
            nc.gpsimd.tensor_tensor(
                out=o_vl[:, 5, :, 16:HD],
                in0=o_vl[:, 5, :, 16:HD],
                in1=bias_vx[:, 0:32].unsqueeze(1).to_broadcast([P, NT, 32]),
                op=ALU.add,
            )
            store(nc.sync, 2, o_vl[:, 6:16], 22, 10)

        def v_product(c):
            vacc = bank("va", 1)
            for g in range(NG):
                nc.tensor.matmul_mx(
                    out=vacc[:],
                    lhsT=wq[2][c // 4][:, g, 256 * (c % 4) : 256 * (c % 4 + 1)].bitcast(E2X4),
                    lhsT_scale=ws[2][:, g, P * c : P * (c + 1)],
                    rhs=xc[:, g * 512 : (g + 1) * 512].bitcast(E5X4),
                    rhs_scale=xs[:, g * 512 : (g + 1) * 512],
                    start=(g == 0),
                    stop=(g == NG - 1),
                )
            vt = work.tile([P, 512], F32, name="vt", tag="vt", bufs=3)
            nc.scalar.activation(out=vt[:], in_=vacc[:], func=ACT.Identity, bias=bcol[:, c : c + 1], scale=1.0)
            vts[c] = vt

        def v_back_pe(c):
            pt = bank("pt", 2)
            for t in range(NT):
                nc.tensor.transpose(pt[:, P * t : P * (t + 1)], vts[c][:, P * t : P * (t + 1)], ident[:])
            return pt

        def v_back_out(c, pt):
            if c % 3 == 0 and c < 6:
                o_new = work.tile([P, 8, NT, HD], F32, name="o_v", tag="o_v", bufs=2)
                ovs[c // 3] = o_new
            o_v = ovs[c // 3]
            pt_v = pt[:].rearrange("p (t f) -> p t f", t=NT)
            col = P * (c % 3)
            end = col + P
            while col < end:
                h = col // HD
                e0 = col % HD
                a0 = col - P * (c % 3)
                if e0 == 0 and end - col >= HD:
                    nh = (end - col) // HD
                    n = nh * HD
                    nc.scalar.copy(
                        out=o_v[:, h : h + nh].rearrange("p h t e -> p t h e"),
                        in_=pt_v[:, :, a0 : a0 + n].rearrange("p t (h e) -> p t h e", e=HD),
                    )
                else:
                    n = min(HD - e0, end - col)
                    nc.scalar.copy(out=o_v[:, h, :, e0 : e0 + n], in_=pt_v[:, :, a0 : a0 + n])
                col += n
            if c % 3 == 2:
                store(nc.scalar, 2, o_v, 8 * (c // 3), 8)
            if c == 7:
                store(nc.scalar, 2, o_v, 16, 6)

        def v_back_pair(c):
            pt0 = v_back_pe(c)
            pt1 = v_back_pe(c + 1)
            v_back_out(c, pt0)
            v_back_out(c + 1, pt1)

        def rotate(which, y_t, dst, h0, p0, p1, t0, t1):
            nc.vector.tensor_tensor(
                out=dst[:, p0:p1, t0:t1, :].rearrange("p h t e -> p t h e"),
                in0=y_t[:, t0:t1, HD * (h0 + p0) : HD * (h0 + p1)].rearrange("p t (h e) -> p t h e", e=HD),
                in1=tabp_v[:, which, t0:t1, :].unsqueeze(2).to_broadcast([P, t1 - t0, p1 - p0, HD]),
                op=ALU.mult,
            )

        def rotate_pool(y_t, dst, h0, p0, p1):
            nc.gpsimd.tensor_tensor(
                out=dst[:, p0:p1].rearrange("p h t e -> p t h e"),
                in0=y_t[:, :, HD * (h0 + p0) : HD * (h0 + p1)].rearrange("p t (h e) -> p t h e", e=HD),
                in1=tab[:, 1].unsqueeze(2).to_broadcast([P, NT, p1 - p0, HD]),
                op=ALU.mult,
            )

        def combine(eng, a_t, b_t, p0, p1):
            a_v = a_t[:, p0:p1].rearrange("p h t (a s i) -> p (h t a) s i", a=3, s=2)
            b_v = b_t[:, p0:p1].rearrange("p h t (a s i) -> p (h t a) s i", a=3, s=2)
            if eng is nc.gpsimd:
                eng.tensor_tensor(out=a_v, in0=a_v, in1=b_v[:, :, ::-1, :], op=ALU.add)
            else:
                for hh in range(2):
                    eng.tensor_tensor(out=a_v[:, :, hh, :], in0=a_v[:, :, hh, :], in1=b_v[:, :, 1 - hh, :], op=ALU.add)

        y_t = work.tile([P, NT, JW], F32, name="y_t", tag="y_t", bufs=1)
        a_t = work.tile([P, 11, NT, HD], F32, name="a_t", tag="a_t", bufs=4)
        b_t = work.tile([P, 11, NT, HD], F32, name="b_t", tag="b_t", bufs=3)
        transpose_x(0, "pt", 2)
        transpose_x(1, "acc", 4)
        spread_bias(0)
        quantise_x(0)
        quantise_x(1)
        qk_group(y_t, 0, 0, 0)
        ptmp = bank("va", 1)
        for k in range(3):
            nc.tensor.transpose(ptmp[:, P * k : P * (k + 1)], tab2[:, P * k : P * (k + 1)], ident[:])
        nc.scalar.copy(out=tabT[:], in_=ptmp[:, 0 : 3 * P])
        qk_group(y_t, 0, 0, 1)
        tabp = bank("tabp", 1)
        for k in range(3):
            nc.tensor.transpose(tabp[:, P * k : P * (k + 1)], tabT[:, P * k : P * (k + 1)], ident[:])
        tabp_v = tabp[:, 0 : 3 * P].rearrange("p (c t e) -> p c t e", c=2, t=NT)
        rotate(0, y_t, a_t, 0, 0, 10, 0, 2)
        transpose_x(2, "pt", 2)
        transpose_x(3, "acc", 4)
        quantise_x(2)
        quantise_x(3)
        zero_plane(1)
        load_scales(1)
        rotate(1, y_t, b_t, 0, 0, 10, 0, 2)
        qk_group(y_t, 0, 0, 2)
        qk_group(y_t, 0, 0, 3)
        rotate(0, y_t, a_t, 0, 0, 10, 2, 4)
        rotate(1, y_t, b_t, 0, 0, 10, 2, 4)
        combine(nc.gpsimd, a_t, b_t, 0, 10)
        store(nc.sync, 0, a_t, 0, 10)
        pbv = spread_bias_pe(8)
        nc.scalar.copy(out=bias_vx[:], in_=pbv[:])
        vx_group(0, "va", 1)
        spread_bias(1)
        vx_group(1, "pt", 2)

        for unit in range(1, 6):
            j = unit // 3
            cl = unit % 3
            if unit == 3:
                y_t = work.tile([P, NT, JW], F32, name="y_t", tag="y_t", bufs=1)
            for t in range(NT):
                qk_group(y_t, j, cl, t)
            if unit == 1:
                vx_group(2, "pt", 2)
                vx_group(3, "va", 1)
                spread_bias(2)
            elif unit == 2:
                pbc = bank("pt", 2)
                nc.tensor.matmul(pbc[:, 0:16], lhsT=bvr[:], rhs=identb[:, 0:16], start=True, stop=True)
                nc.scalar.copy(out=bcol[:], in_=pbc[:, 0:12])
                v_product(0)
                spread_bias(3)
                v_product(1)
            else:
                v_product(2 * unit - 4)
                v_back_pair(2 * unit - 6)
                v_product(2 * unit - 3)
                if unit < 5:
                    spread_bias(unit + 1)
                else:
                    v_back_pair(6)
            h0, h1 = HEADS[cl]
            nh = h1 - h0
            a_t = work.tile([P, 11, NT, HD], F32, name="a_t", tag="a_t", bufs=4)
            b_t = work.tile([P, 11, NT, HD], F32, name="b_t", tag="b_t", bufs=3)
            if unit < 5:
                pool_heads = POOL_HEADS if unit < 3 else 0
                if pool_heads:
                    rotate_pool(y_t, b_t, h0, nh - pool_heads, nh)
                if unit == 2:
                    vx_bias()
                rotate(0, y_t, a_t, h0, 0, nh, 0, NT)
                rotate(1, y_t, b_t, h0, 0, nh - pool_heads, 0, NT)
                combine(nc.gpsimd, a_t, b_t, 0, nh)
                store(nc.sync, j, a_t, h0, nh)
            else:
                rotate(0, y_t, a_t, h0, 0, 6, 0, NT)
                rotate(1, y_t, b_t, h0, 0, 6, 0, NT)
                combine(nc.gpsimd, a_t, b_t, 0, 6)
                store(nc.sync, j, a_t[:, 0:6], h0, 6)
                rotate(0, y_t, a_t, h0, 6, 11, 0, NT)
                rotate(1, y_t, b_t, h0, 6, 11, 0, NT)
                combine(nc.vector, a_t, b_t, 6, 11)
                store(nc.scalar, j, a_t[:, 6:11], h0 + 6, 5)
